import numpy as np
import ml_dtypes


def mxq(x, axis, fmt="e4m3"):
    dtype, down = {"e4m3": (ml_dtypes.float8_e4m3fn, 7), "e5m2": (ml_dtypes.float8_e5m2, 14)}[fmt]
    v = np.moveaxis(np.asarray(x, np.float32).astype(ml_dtypes.bfloat16).astype(np.float64), axis, -1)
    blocks = v.reshape(v.shape[:-1] + (-1, 32))
    amax = np.abs(blocks).max(-1, keepdims=True)
    byte = np.maximum(np.where(amax > 0, np.frexp(amax)[1] - 1 + 127, 0) - down, 1)
    scale = np.exp2(byte - 127.0)
    codes = (blocks / scale).astype(np.float32).astype(dtype).astype(np.float64)
    return np.moveaxis((codes * scale).reshape(v.shape), -1, axis)


WIDE = False


def mx_kscale(k):
    if not WIDE:
        return np.ones(k)
    levels = np.array([10, -10, 5, -5, 0])
    if k % 512:
        return np.exp2(np.random.permutation(np.resize(levels, k // 32))).repeat(32)
    a = np.empty((k // 512, 16))
    for p in range(k // 512):
        a[p, :8] = np.random.permutation(np.resize(levels, 8))
        for g in range(8):
            far = levels[np.abs(levels - a[p, g]) >= 10]
            a[p, g + 8] = far[np.random.randint(len(far))]
    return np.exp2(a.ravel()).repeat(32)


BF16 = ml_dtypes.bfloat16


def bf(x):
    return np.asarray(x, np.float32).astype(BF16)


def f64(x):
    return np.asarray(x).astype(np.float64)


N, H, O, L = 1024, 512, 512, 4


def represent(h):
    n = h.shape[0]
    total = np.sum(h, axis=0, keepdims=True)
    return (n * h - total) / (n - 1)


def sigmoid(v):
    return 1.0 / (1.0 + np.exp(-v))


def setup_inputs():
    t = mx_kscale(H)
    mu = np.random.standard_normal(H)
    return {"h": bf((np.random.standard_normal((N, H)) * 1.2 + mu) * t),
            "w": bf(np.random.standard_normal((H, H)) * 0.6 / np.sqrt(H) * t[:, None] / t[None, :]),
            "w_ff": bf(np.random.standard_normal((O, H)) * 0.6 / np.sqrt(H) / t[None, :]),
            "b_ff": bf(np.random.standard_normal(O) * 0.3)}


def reference(h, w, w_ff, b_ff):
    h = f64(h)
    r = represent(h)
    f = mxq(r, 1, "e4m3") @ mxq(f64(w), 1, "e4m3").T
    h_new = f + h
    return sigmoid((mxq(h_new, 1, "e4m3") @ mxq(f64(w_ff), 1, "e4m3").T) + f64(b_ff))

@@ -1,0 +1,214 @@
+from contextlib import ExitStack
+
+import concourse.mybir as mybir
+from concourse.masks import make_identity
+
+F32 = mybir.dt.float32
+BF16 = mybir.dt.bfloat16
+U32 = mybir.dt.uint32
+U8 = mybir.dt.uint8
+FP8X4 = mybir.dt.float8_e4m3fn_x4
+ALU = mybir.AluOpType
+ACT = mybir.ActivationFunctionType
+
+P = 128
+PACK = 4
+ITEMS = 1024
+HID = 512
+OUT = 512
+ITEM_TILES = ITEMS // P
+HID_TILES = HID // P
+PAIR = 2 * P
+HALF = ITEMS // 2
+SUM_COLS = 32
+QUANTISE_LAG = 1
+SECOND_LAG = 3
+
+FLOPS = 2 * ITEMS * HID * HID + 2 * ITEMS * HID * OUT
+
+
+def tile_differ_amplifier_pa_kernel(tc, h, w, w_ff, b_ff, out):
+    nc = tc.nc
+    with ExitStack() as ctx:
+        keep = ctx.enter_context(tc.tile_pool(name="keep", bufs=1))
+        results = ctx.enter_context(tc.tile_pool(name="results", bufs=ITEM_TILES))
+        banks = ctx.enter_context(tc.psum_pool(name="banks", bufs=7))
+        sum_bank = ctx.enter_context(tc.psum_pool(name="sum_bank", bufs=1))
+        ctx.enter_context(tc.manual_schedule())
+
+        h_sb = keep.tile([P, ITEM_TILES * HID], BF16)
+        h_rows = h.rearrange("(p a) k -> p (a k)", a=ITEM_TILES)
+        for c in range(ITEM_TILES // 2):
+            cols = slice(c * 2 * HID, (c + 1) * 2 * HID)
+            nc.sync.dma_start(out=h_sb[:, cols], in_=h_rows[:, cols])
+        w_sb = keep.tile([P, HID_TILES * HID], BF16)
+        nc.sync.dma_start(
+            out=w_sb[:],
+            in_=w.rearrange("(p t) k -> p (t k)", t=PACK),
+        )
+        wf_sb = keep.tile([P, HID_TILES * HID], BF16)
+        nc.sync.dma_start(
+            out=wf_sb[:].rearrange("p (t k) -> p t k", t=HID_TILES),
+            in_=w_ff.rearrange("(t p) k -> p t k", p=P),
+        )
+        bias = keep.tile([P, OUT], BF16)
+        nc.sync.dma_start(out=bias[:], in_=b_ff.partition_broadcast(P))
+
+        ident = keep.tile([P, P], F32)
+        make_identity(nc, ident[:])
+        pick = keep.tile([P, PACK, SUM_COLS], BF16)
+        nc.vector.memset(pick[:], 0.0)
+        for t in range(PACK):
+            nc.vector.memset(pick[:, t, 8 * t : 8 * t + 8], 1.0)
+        warm = keep.tile([P, 1], F32)
+        nc.vector.memset(warm[:], 0.0)
+        nc.scalar.activation(out=warm[:], in_=warm[:], func=ACT.Sigmoid)
+
+        def transpose_pair(rows_words, grouped_words):
+            bank = banks.tile([P, 2, PAIR], F32, tag="bank")
+            for i in range(2):
+                for u in range(2):
+                    nc.tensor.transpose(
+                        bank[:, u, i * P : (i + 1) * P], rows_words[:, i, u::2], ident[:]
+                    )
+            nc.scalar.copy(out=grouped_words, in_=bank[:].rearrange("p u c -> p c u"))
+
+        def quantise(grouped, codes, scales, first, count):
+            nc.vector.quantize_mx(
+                out=codes[:, first : first + count].bitcast(FP8X4),
+                scales=scales[:, first : first + count],
+                in_=grouped[:, PACK * first : PACK * (first + count)],
+            )
+
+        def words_by_tile(rows, tiles):
+            return rows[:].bitcast(F32).rearrange("p (a q) -> p a q", a=tiles)
+
+        def words_by_column(grouped):
+            return grouped[:].bitcast(F32).rearrange("p (c u) -> p c u", u=2)
+
+        def by_column(grouped):
+            return grouped[:].rearrange("p (c t) -> p c t", t=PACK)
+
+        h_by_value = h_sb[:].rearrange("p (a q t) -> p a t q", a=ITEM_TILES, t=PACK)
+        total = sum_bank.tile([P, SUM_COLS], F32)
+
+        def column_sums(c):
+            for a in (2 * c, 2 * c + 1):
+                for t in range(PACK):
+                    nc.tensor.matmul(
+                        out=total[:],
+                        lhsT=h_by_value[:, a, t, :],
+                        rhs=pick[:, t, :],
+                        start=(a == 0 and t == 0),
+                        stop=(a == ITEM_TILES - 1 and t == PACK - 1),
+                    )
+
+        h_grouped = keep.tile([P, ITEMS * PACK], BF16, align_bytes=64)
+
+        def transpose_h(c):
+            transpose_pair(
+                words_by_tile(h_sb, ITEM_TILES)[:, 2 * c : 2 * c + 2, :],
+                words_by_column(h_grouped)[:, c * PAIR : (c + 1) * PAIR, :],
+            )
+
+        column_sums(0)
+        transpose_h(0)
+        for c in range(1, ITEM_TILES // 2):
+            column_sums(c)
+        for c in range(1, ITEM_TILES // 2):
+            transpose_h(c)
+
+        w_grouped = keep.tile([P, HID * PACK], BF16, align_bytes=64)
+        wf_grouped = keep.tile([P, OUT * PACK], BF16, align_bytes=64)
+        for rows, grouped in ((w_sb, w_grouped), (wf_sb, wf_grouped)):
+            for c in range(HID_TILES // 2):
+                transpose_pair(
+                    words_by_tile(rows, HID_TILES)[:, 2 * c : 2 * c + 2, :],
+                    words_by_column(grouped)[:, c * PAIR : (c + 1) * PAIR, :],
+                )
+        w_codes = keep.tile([P, HID], U32, align_bytes=64)
+        w_scales = keep.tile([P, HID], U8, align_bytes=64)
+        wf_codes = keep.tile([P, OUT], U32, align_bytes=64)
+        wf_scales = keep.tile([P, OUT], U8, align_bytes=64)
+
+        shift = keep.tile([P, PACK], F32)
+        nc.vector.tensor_scalar_mul(
+            out=shift[:],
+            in0=total[:].rearrange("p (t c) -> p t c", t=PACK)[:, :, 0],
+            scalar1=1.0 / (ITEMS - 1),
+        )
+        r_grouped = keep.tile([P, ITEMS * PACK], BF16, align_bytes=64)
+        r_codes = keep.tile([P, ITEMS], U32, align_bytes=64)
+        r_scales = keep.tile([P, ITEMS], U8, align_bytes=64)
+
+        def centre(c):
+            cols = slice(c * PAIR, (c + 1) * PAIR)
+            nc.vector.scalar_tensor_tensor(
+                out=by_column(r_grouped)[:, cols, :],
+                in0=by_column(h_grouped)[:, cols, :],
+                scalar=ITEMS / (ITEMS - 1),
+                in1=shift[:].unsqueeze(1).to_broadcast([P, PAIR, PACK]),
+                op0=ALU.mult,
+                op1=ALU.subtract,
+            )
+
+        centre(0)
+        centre(1)
+        centre(2)
+        quantise(r_grouped, r_codes, r_scales, 0, HALF)
+        centre(3)
+        quantise(w_grouped, w_codes, w_scales, 0, HID)
+        quantise(r_grouped, r_codes, r_scales, HALF, HALF)
+
+        n_grouped = keep.tile([P, ITEMS * PACK], BF16, align_bytes=64)
+        n_codes = keep.tile([P, ITEMS], U32, align_bytes=64)
+        n_scales = keep.tile([P, ITEMS], U8, align_bytes=64)
+
+        def first_product(a):
+            items = slice(a * P, (a + 1) * P)
+            product = banks.tile([P, PACK, P], F32, tag="bank")
+            for t in range(PACK):
+                units = slice(t * P, (t + 1) * P)
+                nc.tensor.matmul_mx(
+                    out=product[:, t, :],
+                    lhsT=w_codes[:, units].bitcast(FP8X4),
+                    lhsT_scale=w_scales[:, units],
+                    rhs=r_codes[:, items].bitcast(FP8X4),
+                    rhs_scale=r_scales[:, items],
+                    start=True,
+                    stop=True,
+                )
+            nc.vector.tensor_tensor(
+                out=by_column(n_grouped)[:, items, :],
+                in0=product[:].rearrange("p t n -> p n t"),
+                in1=by_column(h_grouped)[:, items, :],
+                op=ALU.add,
+            )
+
+        out_rows = out.rearrange("(p a) o -> p a o", a=ITEM_TILES)
+
+        def second_product(a):
+            items = slice(a * P, (a + 1) * P)
+            product = banks.tile([P, OUT], F32, tag="bank")
+            nc.tensor.matmul_mx(
+                out=product[:],
+                lhsT=n_codes[:, items].bitcast(FP8X4),
+                lhsT_scale=n_scales[:, items],
+                rhs=wf_codes[:].bitcast(FP8X4),
+                rhs_scale=wf_scales[:],
+                start=True,
+                stop=True,
+            )
+            result = results.tile([P, OUT], F32)
+            nc.vector.tensor_tensor(out=result[:], in0=product[:], in1=bias[:], op=ALU.add)
+            nc.scalar.activation(out=result[:], in_=result[:], func=ACT.Sigmoid)
+            nc.sync.dma_start(out=out_rows[:, a, :], in_=result[:])
+
+        quantise(wf_grouped, wf_codes, wf_scales, 0, OUT)
+        for step in range(ITEM_TILES + SECOND_LAG):
+            if step < ITEM_TILES:
+                first_product(step)
+            if 0 <= step - QUANTISE_LAG < ITEM_TILES:
+                quantise(n_grouped, n_codes, n_scales, (step - QUANTISE_LAG) * P, P)
+            if 0 <= step - SECOND_LAG:
+                second_product(step - SECOND_LAG)

@@ -21,8 +21,6 @@ HID_TILES = HID // P
 PAIR = 2 * P
 HALF = ITEMS // 2
 SUM_COLS = 32
-QUANTISE_LAG = 1
-SECOND_LAG = 3
 
 FLOPS = 2 * ITEMS * HID * HID + 2 * ITEMS * HID * OUT
 
@@ -42,15 +40,11 @@ def tile_differ_amplifier_pa_kernel(tc, h, w, w_ff, b_ff, out):
             cols = slice(c * 2 * HID, (c + 1) * 2 * HID)
             nc.sync.dma_start(out=h_sb[:, cols], in_=h_rows[:, cols])
         w_sb = keep.tile([P, HID_TILES * HID], BF16)
-        nc.sync.dma_start(
-            out=w_sb[:],
-            in_=w.rearrange("(p t) k -> p (t k)", t=PACK),
-        )
+        nc.sync.dma_start(out=w_sb[:], in_=w.rearrange("(p t) k -> p (t k)", t=PACK))
         wf_sb = keep.tile([P, HID_TILES * HID], BF16)
-        nc.sync.dma_start(
-            out=wf_sb[:].rearrange("p (t k) -> p t k", t=HID_TILES),
-            in_=w_ff.rearrange("(t p) k -> p t k", p=P),
-        )
+        nc.sync.dma_start(out=wf_sb[:], in_=w_ff.rearrange("(p t) k -> p (t k)", t=PACK))
+        bias_col = keep.tile([P, PACK], BF16)
+        nc.sync.dma_start(out=bias_col[:], in_=b_ff.rearrange("(p t) -> p t", t=PACK))
         bias = keep.tile([P, OUT], BF16)
         nc.sync.dma_start(out=bias[:], in_=b_ff.partition_broadcast(P))
 
@@ -68,9 +62,7 @@ def tile_differ_amplifier_pa_kernel(tc, h, w, w_ff, b_ff, out):
             bank = banks.tile([P, 2, PAIR], F32, tag="bank")
             for i in range(2):
                 for u in range(2):
-                    nc.tensor.transpose(
-                        bank[:, u, i * P : (i + 1) * P], rows_words[:, i, u::2], ident[:]
-                    )
+                    nc.tensor.transpose(bank[:, u, i * P : (i + 1) * P], rows_words[:, i, u::2], ident[:])
             nc.scalar.copy(out=grouped_words, in_=bank[:].rearrange("p u c -> p c u"))
 
         def quantise(grouped, codes, scales, first, count):
@@ -104,28 +96,27 @@ def tile_differ_amplifier_pa_kernel(tc, h, w, w_ff, b_ff, out):
                     )
 
         h_grouped = keep.tile([P, ITEMS * PACK], BF16, align_bytes=64)
+        w_grouped = keep.tile([P, HID * PACK], BF16, align_bytes=64)
+        wf_grouped = keep.tile([P, OUT * PACK], BF16, align_bytes=64)
 
-        def transpose_h(c):
+        def transpose_rows(rows, tiles, grouped, c):
             transpose_pair(
-                words_by_tile(h_sb, ITEM_TILES)[:, 2 * c : 2 * c + 2, :],
-                words_by_column(h_grouped)[:, c * PAIR : (c + 1) * PAIR, :],
+                words_by_tile(rows, tiles)[:, 2 * c : 2 * c + 2, :],
+                words_by_column(grouped)[:, c * PAIR : (c + 1) * PAIR, :],
             )
 
         column_sums(0)
-        transpose_h(0)
+        transpose_rows(h_sb, ITEM_TILES, h_grouped, 0)
         for c in range(1, ITEM_TILES // 2):
             column_sums(c)
-        for c in range(1, ITEM_TILES // 2):
-            transpose_h(c)
+        transpose_rows(h_sb, ITEM_TILES, h_grouped, 1)
+        transpose_rows(h_sb, ITEM_TILES, h_grouped, 2)
+        transpose_rows(w_sb, HID_TILES, w_grouped, 0)
+        transpose_rows(w_sb, HID_TILES, w_grouped, 1)
+        transpose_rows(wf_sb, HID_TILES, wf_grouped, 0)
+        transpose_rows(wf_sb, HID_TILES, wf_grouped, 1)
+        transpose_rows(h_sb, ITEM_TILES, h_grouped, 3)
 
-        w_grouped = keep.tile([P, HID * PACK], BF16, align_bytes=64)
-        wf_grouped = keep.tile([P, OUT * PACK], BF16, align_bytes=64)
-        for rows, grouped in ((w_sb, w_grouped), (wf_sb, wf_grouped)):
-            for c in range(HID_TILES // 2):
-                transpose_pair(
-                    words_by_tile(rows, HID_TILES)[:, 2 * c : 2 * c + 2, :],
-                    words_by_column(grouped)[:, c * PAIR : (c + 1) * PAIR, :],
-                )
         w_codes = keep.tile([P, HID], U32, align_bytes=64)
         w_scales = keep.tile([P, HID], U8, align_bytes=64)
         wf_codes = keep.tile([P, OUT], U32, align_bytes=64)
@@ -135,7 +126,7 @@ def tile_differ_amplifier_pa_kernel(tc, h, w, w_ff, b_ff, out):
         nc.vector.tensor_scalar_mul(
             out=shift[:],
             in0=total[:].rearrange("p (t c) -> p t c", t=PACK)[:, :, 0],
-            scalar1=1.0 / (ITEMS - 1),
+            scalar1=-1.0 / (ITEMS - 1),
         )
         r_grouped = keep.tile([P, ITEMS * PACK], BF16, align_bytes=64)
         r_codes = keep.tile([P, ITEMS], U32, align_bytes=64)
@@ -149,20 +140,27 @@ def tile_differ_amplifier_pa_kernel(tc, h, w, w_ff, b_ff, out):
                 scalar=ITEMS / (ITEMS - 1),
                 in1=shift[:].unsqueeze(1).to_broadcast([P, PAIR, PACK]),
                 op0=ALU.mult,
-                op1=ALU.subtract,
+                op1=ALU.add,
             )
 
-        centre(0)
-        centre(1)
-        centre(2)
-        quantise(r_grouped, r_codes, r_scales, 0, HALF)
-        centre(3)
-        quantise(w_grouped, w_codes, w_scales, 0, HID)
-        quantise(r_grouped, r_codes, r_scales, HALF, HALF)
+        centred = keep.tile([P, PACK, PAIR], BF16)
+
+        def centre_on_scalar(c):
+            cols = slice(c * PAIR, (c + 1) * PAIR)
+            for t in range(PACK):
+                nc.scalar.activation(
+                    out=centred[:, t, :],
+                    in_=by_column(h_grouped)[:, cols, t],
+                    func=ACT.Identity,
+                    scale=ITEMS / (ITEMS - 1),
+                    bias=shift[:, t : t + 1],
+                )
+            nc.scalar.copy(out=by_column(r_grouped)[:, cols, :], in_=centred[:].rearrange("p t c -> p c t"))
 
         n_grouped = keep.tile([P, ITEMS * PACK], BF16, align_bytes=64)
         n_codes = keep.tile([P, ITEMS], U32, align_bytes=64)
         n_scales = keep.tile([P, ITEMS], U8, align_bytes=64)
+        first_products = {}
 
         def first_product(a):
             items = slice(a * P, (a + 1) * P)
@@ -178,16 +176,66 @@ def tile_differ_amplifier_pa_kernel(tc, h, w, w_ff, b_ff, out):
                     start=True,
                     stop=True,
                 )
+            first_products[a] = product
+
+        def residual_add(a):
+            items = slice(a * P, (a + 1) * P)
             nc.vector.tensor_tensor(
                 out=by_column(n_grouped)[:, items, :],
-                in0=product[:].rearrange("p t n -> p n t"),
+                in0=first_products[a][:].rearrange("p t n -> p n t"),
                 in1=by_column(h_grouped)[:, items, :],
                 op=ALU.add,
             )
 
         out_rows = out.rearrange("(p a) o -> p a o", a=ITEM_TILES)
+        activated = {}
 
-        def second_product(a):
+        def second_product_by_channel(g):
+            items = slice(g * PAIR, (g + 1) * PAIR)
+            act = keep.tile([P, PACK, PAIR], F32, name="act%d" % g)
+            for half in range(2):
+                product = banks.tile([P, 2, PAIR], F32, tag="bank")
+                for i in range(2):
+                    t = 2 * half + i
+                    channels = slice(t * P, (t + 1) * P)
+                    nc.tensor.matmul_mx(
+                        out=product[:, i, :],
+                        lhsT=wf_codes[:, channels].bitcast(FP8X4),
+                        lhsT_scale=wf_scales[:, channels],
+                        rhs=n_codes[:, items].bitcast(FP8X4),
+                        rhs_scale=n_scales[:, items],
+                        start=True,
+                        stop=True,
+                    )
+                for i in range(2):
+                    t = 2 * half + i
+                    nc.scalar.activation(
+                        out=act[:, t, :], in_=product[:, i, :], func=ACT.Sigmoid, bias=bias_col[:, t : t + 1]
+                    )
+            activated[g] = act
+
+        turned = {}
+
+        def turn(g):
+            for a in (2 * g, 2 * g + 1):
+                columns = slice((a - 2 * g) * P, (a - 2 * g + 1) * P)
+                rows = banks.tile([P, PACK, P], F32, tag="bank")
+                for t in range(PACK):
+                    nc.tensor.transpose(rows[:, t, :], activated[g][:, t, columns], ident[:])
+                turned[a] = rows
+
+        def store_turned(g):
+            for a in (2 * g, 2 * g + 1):
+                result = results.tile([P, OUT], F32)
+                nc.scalar.copy(
+                    out=result[:].rearrange("p (m t) -> p m t", t=PACK),
+                    in_=turned[a][:].rearrange("p t m -> p m t"),
+                )
+                nc.sync.dma_start(out=out_rows[:, a, :], in_=result[:])
+
+        second_products = {}
+
+        def second_product_by_item(a):
             items = slice(a * P, (a + 1) * P)
             product = banks.tile([P, OUT], F32, tag="bank")
             nc.tensor.matmul_mx(
@@ -199,16 +247,59 @@ def tile_differ_amplifier_pa_kernel(tc, h, w, w_ff, b_ff, out):
                 start=True,
                 stop=True,
             )
+            second_products[a] = product
+
+        def finish(a):
             result = results.tile([P, OUT], F32)
-            nc.vector.tensor_tensor(out=result[:], in0=product[:], in1=bias[:], op=ALU.add)
+            nc.vector.tensor_tensor(
+                out=result[:].rearrange("p (m t) -> p m t", t=PACK),
+                in0=second_products[a][:].rearrange("p (t m) -> p m t", t=PACK),
+                in1=bias[:].rearrange("p (m t) -> p m t", t=PACK),
+                op=ALU.add,
+            )
             nc.scalar.activation(out=result[:], in_=result[:], func=ACT.Sigmoid)
             nc.sync.dma_start(out=out_rows[:, a, :], in_=result[:])
 
+        def quantise_pair(g):
+            quantise(n_grouped, n_codes, n_scales, g * PAIR, PAIR)
+
+        centre(0)
+        centre(1)
+        quantise(r_grouped, r_codes, r_scales, 0, HALF)
+        quantise(w_grouped, w_codes, w_scales, 0, HID)
         quantise(wf_grouped, wf_codes, wf_scales, 0, OUT)
-        for step in range(ITEM_TILES + SECOND_LAG):
-            if step < ITEM_TILES:
-                first_product(step)
-            if 0 <= step - QUANTISE_LAG < ITEM_TILES:
-                quantise(n_grouped, n_codes, n_scales, (step - QUANTISE_LAG) * P, P)
-            if 0 <= step - SECOND_LAG:
-                second_product(step - SECOND_LAG)
+        centre_on_scalar(3)
+        for a in range(4):
+            first_product(a)
+        residual_add(0)
+        residual_add(1)
+        centre(2)
+        quantise_pair(0)
+        second_product_by_channel(0)
+        quantise(r_grouped, r_codes, r_scales, HALF, HALF)
+        residual_add(2)
+        first_product(4)
+        first_product(5)
+        residual_add(3)
+        turn(0)
+        store_turned(0)
+        residual_add(4)
+        quantise_pair(1)
+        first_product(6)
+        second_product_by_channel(1)
+        first_product(7)
+        residual_add(5)
+        residual_add(6)
+        quantise_pair(2)
+        second_product_by_item(4)
+        second_product_by_item(5)
+        turn(1)
+        residual_add(7)
+        finish(4)
+        store_turned(1)
+        quantise_pair(3)
+        second_product_by_item(6)
+        second_product_by_item(7)
+        finish(5)
+        finish(6)
+        finish(7)

@@ -20,6 +20,7 @@ ITEM_TILES = ITEMS // P
 HID_TILES = HID // P
 PAIR = 2 * P
 HALF = ITEMS // 2
+WARM_MATMULS = 3
 SUM_COLS = 32
 
 FLOPS = 2 * ITEMS * HID * HID + 2 * ITEMS * HID * OUT
@@ -48,6 +49,8 @@ def tile_differ_amplifier_pa_kernel(tc, h, w, w_ff, b_ff, out):
         bias = keep.tile([P, OUT], BF16)
         nc.sync.dma_start(out=bias[:], in_=b_ff.partition_broadcast(P))
 
+        zeros = keep.tile([P, P], F32)
+        nc.vector.memset(zeros[:], 0.0)
         ident = keep.tile([P, P], F32)
         make_identity(nc, ident[:])
         pick = keep.tile([P, PACK, SUM_COLS], BF16)
@@ -105,16 +108,20 @@ def tile_differ_amplifier_pa_kernel(tc, h, w, w_ff, b_ff, out):
                 words_by_column(grouped)[:, c * PAIR : (c + 1) * PAIR, :],
             )
 
+        idle = banks.tile([P, P], F32, tag="bank", name="idle")
+        for i in range(WARM_MATMULS):
+            nc.tensor.matmul(out=idle[:], lhsT=zeros[:], rhs=zeros[:], start=True, stop=True)
         column_sums(0)
         transpose_rows(h_sb, ITEM_TILES, h_grouped, 0)
-        for c in range(1, ITEM_TILES // 2):
-            column_sums(c)
+        column_sums(1)
+        column_sums(2)
+        column_sums(3)
         transpose_rows(h_sb, ITEM_TILES, h_grouped, 1)
-        transpose_rows(h_sb, ITEM_TILES, h_grouped, 2)
         transpose_rows(w_sb, HID_TILES, w_grouped, 0)
         transpose_rows(w_sb, HID_TILES, w_grouped, 1)
         transpose_rows(wf_sb, HID_TILES, wf_grouped, 0)
         transpose_rows(wf_sb, HID_TILES, wf_grouped, 1)
+        transpose_rows(h_sb, ITEM_TILES, h_grouped, 2)
         transpose_rows(h_sb, ITEM_TILES, h_grouped, 3)
 
         w_codes = keep.tile([P, HID], U32, align_bytes=64)
@@ -132,13 +139,13 @@ def tile_differ_amplifier_pa_kernel(tc, h, w, w_ff, b_ff, out):
         r_codes = keep.tile([P, ITEMS], U32, align_bytes=64)
         r_scales = keep.tile([P, ITEMS], U8, align_bytes=64)
 
-        def centre(c):
-            cols = slice(c * PAIR, (c + 1) * PAIR)
+        def centre(first, count):
+            cols = slice(first * P, (first + count) * P)
             nc.vector.scalar_tensor_tensor(
                 out=by_column(r_grouped)[:, cols, :],
                 in0=by_column(h_grouped)[:, cols, :],
                 scalar=ITEMS / (ITEMS - 1),
-                in1=shift[:].unsqueeze(1).to_broadcast([P, PAIR, PACK]),
+                in1=shift[:].unsqueeze(1).to_broadcast([P, count * P, PACK]),
                 op0=ALU.mult,
                 op1=ALU.add,
             )
@@ -224,14 +231,13 @@ def tile_differ_amplifier_pa_kernel(tc, h, w, w_ff, b_ff, out):
                     nc.tensor.transpose(rows[:, t, :], activated[g][:, t, columns], ident[:])
                 turned[a] = rows
 
-        def store_turned(g):
-            for a in (2 * g, 2 * g + 1):
-                result = results.tile([P, OUT], F32)
-                nc.scalar.copy(
-                    out=result[:].rearrange("p (m t) -> p m t", t=PACK),
-                    in_=turned[a][:].rearrange("p t m -> p m t"),
-                )
-                nc.sync.dma_start(out=out_rows[:, a, :], in_=result[:])
+        def store_turned(a, copy):
+            result = results.tile([P, OUT], F32)
+            copy(
+                out=result[:].rearrange("p (m t) -> p m t", t=PACK),
+                in_=turned[a][:].rearrange("p t m -> p m t"),
+            )
+            nc.sync.dma_start(out=out_rows[:, a, :], in_=result[:])
 
         second_products = {}
 
@@ -263,17 +269,19 @@ def tile_differ_amplifier_pa_kernel(tc, h, w, w_ff, b_ff, out):
         def quantise_pair(g):
             quantise(n_grouped, n_codes, n_scales, g * PAIR, PAIR)
 
-        centre(0)
-        centre(1)
-        quantise(r_grouped, r_codes, r_scales, 0, HALF)
-        quantise(w_grouped, w_codes, w_scales, 0, HID)
-        quantise(wf_grouped, wf_codes, wf_scales, 0, OUT)
         centre_on_scalar(3)
-        for a in range(4):
-            first_product(a)
+        centre(0, 2)
+        centre(2, 2)
+        quantise(w_grouped, w_codes, w_scales, 0, HID)
+        quantise(r_grouped, r_codes, r_scales, 0, HALF)
+        quantise(wf_grouped, wf_codes, wf_scales, 0, OUT)
+        first_product(0)
+        first_product(1)
+        first_product(2)
+        first_product(3)
         residual_add(0)
         residual_add(1)
-        centre(2)
+        centre(4, 2)
         quantise_pair(0)
         second_product_by_channel(0)
         quantise(r_grouped, r_codes, r_scales, HALF, HALF)
@@ -282,7 +290,8 @@ def tile_differ_amplifier_pa_kernel(tc, h, w, w_ff, b_ff, out):
         first_product(5)
         residual_add(3)
         turn(0)
-        store_turned(0)
+        store_turned(0, nc.scalar.copy)
+        store_turned(1, nc.scalar.copy)
         residual_add(4)
         quantise_pair(1)
         first_product(6)
@@ -296,10 +305,11 @@ def tile_differ_amplifier_pa_kernel(tc, h, w, w_ff, b_ff, out):
         turn(1)
         residual_add(7)
         finish(4)
-        store_turned(1)
+        store_turned(2, nc.scalar.copy)
         quantise_pair(3)
         second_product_by_item(6)
         second_product_by_item(7)
         finish(5)
+        store_turned(3, nc.vector.tensor_copy)
         finish(6)
         finish(7)

@@ -31,8 +31,9 @@ def tile_differ_amplifier_pa_kernel(tc, h, w, w_ff, b_ff, out):
     with ExitStack() as ctx:
         keep = ctx.enter_context(tc.tile_pool(name="keep", bufs=1))
         results = ctx.enter_context(tc.tile_pool(name="results", bufs=ITEM_TILES))
-        banks = ctx.enter_context(tc.psum_pool(name="banks", bufs=7))
-        sum_bank = ctx.enter_context(tc.psum_pool(name="sum_bank", bufs=1))
+        middle = ctx.enter_context(tc.tile_pool(name="middle", bufs=2))
+        front = ctx.enter_context(tc.psum_pool(name="front", bufs=4))
+        back = ctx.enter_context(tc.psum_pool(name="back", bufs=4))
         ctx.enter_context(tc.manual_schedule())
 
         h_sb = keep.tile([P, ITEM_TILES * HID], BF16)
@@ -61,12 +62,18 @@ def tile_differ_amplifier_pa_kernel(tc, h, w, w_ff, b_ff, out):
         nc.vector.memset(warm[:], 0.0)
         nc.scalar.activation(out=warm[:], in_=warm[:], func=ACT.Sigmoid)
 
-        def transpose_pair(rows_words, grouped_words):
-            bank = banks.tile([P, 2, PAIR], F32, tag="bank")
+        def transpose_pair(pool, rows_words):
+            bank = pool.tile([P, 2, PAIR], F32, tag="bank", name="words")
             for i in range(2):
                 for u in range(2):
                     nc.tensor.transpose(bank[:, u, i * P : (i + 1) * P], rows_words[:, i, u::2], ident[:])
-            nc.scalar.copy(out=grouped_words, in_=bank[:].rearrange("p u c -> p c u"))
+            return bank
+
+        def copy_grouped(bank, grouped, c):
+            nc.scalar.copy(
+                out=words_by_column(grouped)[:, c * PAIR : (c + 1) * PAIR, :],
+                in_=bank[:].rearrange("p u c -> p c u"),
+            )
 
         def quantise(grouped, codes, scales, first, count):
             nc.vector.quantize_mx(
@@ -85,9 +92,8 @@ def tile_differ_amplifier_pa_kernel(tc, h, w, w_ff, b_ff, out):
             return grouped[:].rearrange("p (c t) -> p c t", t=PACK)
 
         h_by_value = h_sb[:].rearrange("p (a q t) -> p a t q", a=ITEM_TILES, t=PACK)
-        total = sum_bank.tile([P, SUM_COLS], F32)
 
-        def column_sums(c):
+        def column_sums(total, c):
             for a in (2 * c, 2 * c + 1):
                 for t in range(PACK):
                     nc.tensor.matmul(
@@ -102,39 +108,12 @@ def tile_differ_amplifier_pa_kernel(tc, h, w, w_ff, b_ff, out):
         w_grouped = keep.tile([P, HID * PACK], BF16, align_bytes=64)
         wf_grouped = keep.tile([P, OUT * PACK], BF16, align_bytes=64)
 
-        def transpose_rows(rows, tiles, grouped, c):
-            transpose_pair(
-                words_by_tile(rows, tiles)[:, 2 * c : 2 * c + 2, :],
-                words_by_column(grouped)[:, c * PAIR : (c + 1) * PAIR, :],
-            )
-
-        idle = banks.tile([P, P], F32, tag="bank", name="idle")
-        for i in range(WARM_MATMULS):
-            nc.tensor.matmul(out=idle[:], lhsT=zeros[:], rhs=zeros[:], start=True, stop=True)
-        column_sums(0)
-        transpose_rows(h_sb, ITEM_TILES, h_grouped, 0)
-        column_sums(1)
-        column_sums(2)
-        column_sums(3)
-        transpose_rows(h_sb, ITEM_TILES, h_grouped, 1)
-        transpose_rows(w_sb, HID_TILES, w_grouped, 0)
-        transpose_rows(w_sb, HID_TILES, w_grouped, 1)
-        transpose_rows(wf_sb, HID_TILES, wf_grouped, 0)
-        transpose_rows(wf_sb, HID_TILES, wf_grouped, 1)
-        transpose_rows(h_sb, ITEM_TILES, h_grouped, 2)
-        transpose_rows(h_sb, ITEM_TILES, h_grouped, 3)
-
         w_codes = keep.tile([P, HID], U32, align_bytes=64)
         w_scales = keep.tile([P, HID], U8, align_bytes=64)
         wf_codes = keep.tile([P, OUT], U32, align_bytes=64)
         wf_scales = keep.tile([P, OUT], U8, align_bytes=64)
 
         shift = keep.tile([P, PACK], F32)
-        nc.vector.tensor_scalar_mul(
-            out=shift[:],
-            in0=total[:].rearrange("p (t c) -> p t c", t=PACK)[:, :, 0],
-            scalar1=-1.0 / (ITEMS - 1),
-        )
         r_grouped = keep.tile([P, ITEMS * PACK], BF16, align_bytes=64)
         r_codes = keep.tile([P, ITEMS], U32, align_bytes=64)
         r_scales = keep.tile([P, ITEMS], U8, align_bytes=64)
@@ -150,18 +129,33 @@ def tile_differ_amplifier_pa_kernel(tc, h, w, w_ff, b_ff, out):
                 op1=ALU.add,
             )
 
-        centred = keep.tile([P, PACK, PAIR], BF16)
-
-        def centre_on_scalar(c):
-            cols = slice(c * PAIR, (c + 1) * PAIR)
+        def centre_on_scalar(bank):
+            centred = middle.tile([P, PACK, PAIR], BF16, name="centred")
+            values = bank[:].rearrange("p u c -> p (u c)").bitcast(BF16).rearrange("p (u c e) -> p u e c", u=2, e=2)
             for t in range(PACK):
                 nc.scalar.activation(
                     out=centred[:, t, :],
-                    in_=by_column(h_grouped)[:, cols, t],
+                    in_=values[:, t // 2, t % 2, :],
                     func=ACT.Identity,
                     scale=ITEMS / (ITEMS - 1),
                     bias=shift[:, t : t + 1],
                 )
+            return centred
+
+        def interleave_on_gpsimd(centred, c):
+            for i in range(2):
+                columns = slice(i * P, (i + 1) * P)
+                nc.gpsimd.tensor_scalar(
+                    out=by_column(r_grouped)[:, c * PAIR + i * P : c * PAIR + (i + 1) * P, :],
+                    in0=centred[:, :, columns].rearrange("p t c -> p c t"),
+                    scalar1=1.0,
+                    scalar2=0.0,
+                    op0=ALU.mult,
+                    op1=ALU.add,
+                )
+
+        def interleave_on_scalar(centred, c):
+            cols = slice(c * PAIR, (c + 1) * PAIR)
             nc.scalar.copy(out=by_column(r_grouped)[:, cols, :], in_=centred[:].rearrange("p t c -> p c t"))
 
         n_grouped = keep.tile([P, ITEMS * PACK], BF16, align_bytes=64)
@@ -171,7 +165,7 @@ def tile_differ_amplifier_pa_kernel(tc, h, w, w_ff, b_ff, out):
 
         def first_product(a):
             items = slice(a * P, (a + 1) * P)
-            product = banks.tile([P, PACK, P], F32, tag="bank")
+            product = front.tile([P, PACK, P], F32, tag="bank")
             for t in range(PACK):
                 units = slice(t * P, (t + 1) * P)
                 nc.tensor.matmul_mx(
@@ -201,7 +195,7 @@ def tile_differ_amplifier_pa_kernel(tc, h, w, w_ff, b_ff, out):
             items = slice(g * PAIR, (g + 1) * PAIR)
             act = keep.tile([P, PACK, PAIR], F32, name="act%d" % g)
             for half in range(2):
-                product = banks.tile([P, 2, PAIR], F32, tag="bank")
+                product = back.tile([P, 2, PAIR], F32, tag="bank")
                 for i in range(2):
                     t = 2 * half + i
                     channels = slice(t * P, (t + 1) * P)
@@ -226,7 +220,7 @@ def tile_differ_amplifier_pa_kernel(tc, h, w, w_ff, b_ff, out):
         def turn(g):
             for a in (2 * g, 2 * g + 1):
                 columns = slice((a - 2 * g) * P, (a - 2 * g + 1) * P)
-                rows = banks.tile([P, PACK, P], F32, tag="bank")
+                rows = back.tile([P, PACK, P], F32, tag="bank")
                 for t in range(PACK):
                     nc.tensor.transpose(rows[:, t, :], activated[g][:, t, columns], ident[:])
                 turned[a] = rows
@@ -243,7 +237,7 @@ def tile_differ_amplifier_pa_kernel(tc, h, w, w_ff, b_ff, out):
 
         def second_product_by_item(a):
             items = slice(a * P, (a + 1) * P)
-            product = banks.tile([P, OUT], F32, tag="bank")
+            product = front.tile([P, OUT], F32, tag="bank")
             nc.tensor.matmul_mx(
                 out=product[:],
                 lhsT=n_codes[:, items].bitcast(FP8X4),
@@ -269,47 +263,78 @@ def tile_differ_amplifier_pa_kernel(tc, h, w, w_ff, b_ff, out):
         def quantise_pair(g):
             quantise(n_grouped, n_codes, n_scales, g * PAIR, PAIR)
 
-        centre_on_scalar(3)
+        idle = front.tile([P, P], F32, tag="bank", name="idle")
+        for i in range(3):
+            nc.tensor.matmul(out=idle[:], lhsT=zeros[:], rhs=zeros[:], start=True, stop=True)
+        total = front.tile([P, SUM_COLS], F32, tag="bank", name="total")
+        column_sums(total, 0)
+        h_bank_0 = transpose_pair(front, words_by_tile(h_sb, ITEM_TILES)[:, 0 : 2, :])
+        copy_grouped(h_bank_0, h_grouped, 0)
+        column_sums(total, 1)
+        column_sums(total, 2)
+        column_sums(total, 3)
+        nc.vector.tensor_scalar_mul(
+            out=shift[:],
+            in0=total[:].rearrange("p (t c) -> p t c", t=PACK)[:, :, 0],
+            scalar1=-1.0 / (ITEMS - 1),
+        )
+        h_bank_1 = transpose_pair(back, words_by_tile(h_sb, ITEM_TILES)[:, 2 : 4, :])
+        copy_grouped(h_bank_1, h_grouped, 1)
         centre(0, 2)
+        w_bank_0 = transpose_pair(front, words_by_tile(w_sb, HID_TILES)[:, 0 : 2, :])
+        copy_grouped(w_bank_0, w_grouped, 0)
+        w_bank_1 = transpose_pair(front, words_by_tile(w_sb, HID_TILES)[:, 2 : 4, :])
+        copy_grouped(w_bank_1, w_grouped, 1)
+        f_bank_0 = transpose_pair(front, words_by_tile(wf_sb, HID_TILES)[:, 0 : 2, :])
+        copy_grouped(f_bank_0, wf_grouped, 0)
+        f_bank_1 = transpose_pair(front, words_by_tile(wf_sb, HID_TILES)[:, 2 : 4, :])
+        copy_grouped(f_bank_1, wf_grouped, 1)
+        h_bank_2 = transpose_pair(back, words_by_tile(h_sb, ITEM_TILES)[:, 4 : 6, :])
+        h_bank_3 = transpose_pair(back, words_by_tile(h_sb, ITEM_TILES)[:, 6 : 8, :])
         centre(2, 2)
+        copy_grouped(h_bank_2, h_grouped, 2)
+        centred_3 = centre_on_scalar(h_bank_3)
+        interleave_on_gpsimd(centred_3, 3)
         quantise(w_grouped, w_codes, w_scales, 0, HID)
         quantise(r_grouped, r_codes, r_scales, 0, HALF)
-        quantise(wf_grouped, wf_codes, wf_scales, 0, OUT)
         first_product(0)
         first_product(1)
         first_product(2)
         first_product(3)
+        quantise(wf_grouped, wf_codes, wf_scales, 0, OUT)
+        centre(4, 2)
+        copy_grouped(h_bank_3, h_grouped, 3)
         residual_add(0)
         residual_add(1)
-        centre(4, 2)
+        residual_add(2)
         quantise_pair(0)
         second_product_by_channel(0)
-        quantise(r_grouped, r_codes, r_scales, HALF, HALF)
-        residual_add(2)
-        first_product(4)
-        first_product(5)
+        quantise(r_grouped, r_codes, r_scales, 3 * PAIR, PAIR)
+        first_product(6)
+        first_product(7)
         residual_add(3)
+        quantise(r_grouped, r_codes, r_scales, 2 * PAIR, PAIR)
+        first_product(4)
         turn(0)
         store_turned(0, nc.scalar.copy)
         store_turned(1, nc.scalar.copy)
-        residual_add(4)
         quantise_pair(1)
-        first_product(6)
+        first_product(5)
         second_product_by_channel(1)
-        first_product(7)
-        residual_add(5)
         residual_add(6)
-        quantise_pair(2)
-        second_product_by_item(4)
-        second_product_by_item(5)
-        turn(1)
         residual_add(7)
-        finish(4)
-        store_turned(2, nc.scalar.copy)
         quantise_pair(3)
+        residual_add(4)
         second_product_by_item(6)
         second_product_by_item(7)
-        finish(5)
-        store_turned(3, nc.vector.tensor_copy)
+        residual_add(5)
+        turn(1)
         finish(6)
+        quantise_pair(2)
+        store_turned(2, nc.scalar.copy)
+        second_product_by_item(4)
+        second_product_by_item(5)
         finish(7)
+        store_turned(3, nc.vector.tensor_copy)
+        finish(4)
+        finish(5)

@@ -129,34 +129,37 @@ def tile_differ_amplifier_pa_kernel(tc, h, w, w_ff, b_ff, out):
                 op1=ALU.add,
             )
 
-        def centre_on_scalar(bank):
+        def centre_on_scalar(bank, first, count):
             centred = middle.tile([P, PACK, PAIR], BF16, name="centred")
             values = bank[:].rearrange("p u c -> p (u c)").bitcast(BF16).rearrange("p (u c e) -> p u e c", u=2, e=2)
+            start = first % 2 * P
             for t in range(PACK):
                 nc.scalar.activation(
-                    out=centred[:, t, :],
-                    in_=values[:, t // 2, t % 2, :],
+                    out=centred[:, t, : count * P],
+                    in_=values[:, t // 2, t % 2, start : start + count * P],
                     func=ACT.Identity,
                     scale=ITEMS / (ITEMS - 1),
                     bias=shift[:, t : t + 1],
                 )
             return centred
 
-        def interleave_on_gpsimd(centred, c):
-            for i in range(2):
-                columns = slice(i * P, (i + 1) * P)
+        def interleave_on_gpsimd(centred, first, count):
+            for i in range(count):
+                items = slice((first + i) * P, (first + i + 1) * P)
                 nc.gpsimd.tensor_scalar(
-                    out=by_column(r_grouped)[:, c * PAIR + i * P : c * PAIR + (i + 1) * P, :],
-                    in0=centred[:, :, columns].rearrange("p t c -> p c t"),
+                    out=by_column(r_grouped)[:, items, :],
+                    in0=centred[:, :, i * P : (i + 1) * P].rearrange("p t c -> p c t"),
                     scalar1=1.0,
                     scalar2=0.0,
                     op0=ALU.mult,
                     op1=ALU.add,
                 )
 
-        def interleave_on_scalar(centred, c):
-            cols = slice(c * PAIR, (c + 1) * PAIR)
-            nc.scalar.copy(out=by_column(r_grouped)[:, cols, :], in_=centred[:].rearrange("p t c -> p c t"))
+        def interleave_on_scalar(centred, first, count):
+            items = slice(first * P, (first + count) * P)
+            nc.scalar.copy(
+                out=by_column(r_grouped)[:, items, :], in_=centred[:, :, : count * P].rearrange("p t c -> p c t")
+            )
 
         n_grouped = keep.tile([P, ITEMS * PACK], BF16, align_bytes=64)
         n_codes = keep.tile([P, ITEMS], U32, align_bytes=64)
@@ -235,9 +238,9 @@ def tile_differ_amplifier_pa_kernel(tc, h, w, w_ff, b_ff, out):
 
         second_products = {}
 
-        def second_product_by_item(a):
+        def second_product_by_item(a, pool):
             items = slice(a * P, (a + 1) * P)
-            product = front.tile([P, OUT], F32, tag="bank")
+            product = pool.tile([P, OUT], F32, tag="bank")
             nc.tensor.matmul_mx(
                 out=product[:],
                 lhsT=n_codes[:, items].bitcast(FP8X4),
@@ -289,12 +292,11 @@ def tile_differ_amplifier_pa_kernel(tc, h, w, w_ff, b_ff, out):
         copy_grouped(f_bank_0, wf_grouped, 0)
         f_bank_1 = transpose_pair(front, words_by_tile(wf_sb, HID_TILES)[:, 2 : 4, :])
         copy_grouped(f_bank_1, wf_grouped, 1)
-        h_bank_2 = transpose_pair(back, words_by_tile(h_sb, ITEM_TILES)[:, 4 : 6, :])
         h_bank_3 = transpose_pair(back, words_by_tile(h_sb, ITEM_TILES)[:, 6 : 8, :])
+        h_bank_2 = transpose_pair(back, words_by_tile(h_sb, ITEM_TILES)[:, 4 : 6, :])
         centre(2, 2)
-        copy_grouped(h_bank_2, h_grouped, 2)
-        centred_3 = centre_on_scalar(h_bank_3)
-        interleave_on_gpsimd(centred_3, 3)
+        centred_6 = centre_on_scalar(h_bank_3, 6, 2)
+        interleave_on_gpsimd(centred_6, 6, 2)
         quantise(w_grouped, w_codes, w_scales, 0, HID)
         quantise(r_grouped, r_codes, r_scales, 0, HALF)
         first_product(0)
@@ -302,39 +304,42 @@ def tile_differ_amplifier_pa_kernel(tc, h, w, w_ff, b_ff, out):
         first_product(2)
         first_product(3)
         quantise(wf_grouped, wf_codes, wf_scales, 0, OUT)
-        centre(4, 2)
+        copy_grouped(h_bank_2, h_grouped, 2)
         copy_grouped(h_bank_3, h_grouped, 3)
+        centred_t5 = centre_on_scalar(h_bank_2, 5, 1)
+        interleave_on_scalar(centred_t5, 5, 1)
         residual_add(0)
         residual_add(1)
         residual_add(2)
         quantise_pair(0)
         second_product_by_channel(0)
+        residual_add(3)
         quantise(r_grouped, r_codes, r_scales, 3 * PAIR, PAIR)
         first_product(6)
+        quantise_pair(1)
+        second_product_by_channel(1)
         first_product(7)
-        residual_add(3)
-        quantise(r_grouped, r_codes, r_scales, 2 * PAIR, PAIR)
-        first_product(4)
+        centre(4, 1)
+        residual_add(6)
         turn(0)
         store_turned(0, nc.scalar.copy)
         store_turned(1, nc.scalar.copy)
-        quantise_pair(1)
+        quantise(r_grouped, r_codes, r_scales, 2 * PAIR, PAIR)
+        first_product(4)
         first_product(5)
-        second_product_by_channel(1)
-        residual_add(6)
         residual_add(7)
         quantise_pair(3)
         residual_add(4)
-        second_product_by_item(6)
-        second_product_by_item(7)
-        residual_add(5)
+        second_product_by_item(6, front)
         turn(1)
+        store_turned(2, nc.scalar.copy)
+        store_turned(3, nc.scalar.copy)
+        second_product_by_item(7, front)
+        residual_add(5)
         finish(6)
         quantise_pair(2)
-        store_turned(2, nc.scalar.copy)
-        second_product_by_item(4)
-        second_product_by_item(5)
+        second_product_by_item(4, front)
+        second_product_by_item(5, front)
         finish(7)
-        store_turned(3, nc.vector.tensor_copy)
         finish(4)
         finish(5)

@@ -42,9 +42,9 @@ def tile_differ_amplifier_pa_kernel(tc, h, w, w_ff, b_ff, out):
             cols = slice(c * 2 * HID, (c + 1) * 2 * HID)
             nc.sync.dma_start(out=h_sb[:, cols], in_=h_rows[:, cols])
         w_sb = keep.tile([P, HID_TILES * HID], BF16)
-        nc.sync.dma_start(out=w_sb[:], in_=w.rearrange("(p t) k -> p (t k)", t=PACK))
         wf_sb = keep.tile([P, HID_TILES * HID], BF16)
-        nc.sync.dma_start(out=wf_sb[:], in_=w_ff.rearrange("(p t) k -> p (t k)", t=PACK))
+        for rows, source in ((w_sb, w), (wf_sb, w_ff)):
+            nc.sync.dma_start(out=rows[:], in_=source.rearrange("(p t) k -> p (t k)", t=PACK))
         bias_col = keep.tile([P, PACK], BF16)
         nc.sync.dma_start(out=bias_col[:], in_=b_ff.rearrange("(p t) -> p t", t=PACK))
         bias = keep.tile([P, OUT], BF16)
@@ -62,12 +62,17 @@ def tile_differ_amplifier_pa_kernel(tc, h, w, w_ff, b_ff, out):
         nc.vector.memset(warm[:], 0.0)
         nc.scalar.activation(out=warm[:], in_=warm[:], func=ACT.Sigmoid)
 
-        def transpose_pair(pool, rows_words):
+        def transpose_pair(pool, rows_words, idle_matmuls=0):
             bank = pool.tile([P, 2, PAIR], F32, tag="bank", name="words")
+            keep_warm(bank[:, 0, :P], idle_matmuls)
             for i in range(2):
                 for u in range(2):
-                    nc.tensor.transpose(bank[:, u, i * P : (i + 1) * P], rows_words[:, i, u::2], ident[:])
+                    nc.tensor.transpose(bank[:, u, i * P : (i + 1) * P], rows_words[:, i, u, :], ident[:])
             return bank
+
+        def keep_warm(bank, count):
+            for i in range(count):
+                nc.tensor.matmul(out=bank, lhsT=zeros[:], rhs=zeros[:], start=True, stop=True)
 
         def copy_grouped(bank, grouped, c):
             nc.scalar.copy(
@@ -83,7 +88,7 @@ def tile_differ_amplifier_pa_kernel(tc, h, w, w_ff, b_ff, out):
             )
 
         def words_by_tile(rows, tiles):
-            return rows[:].bitcast(F32).rearrange("p (a q) -> p a q", a=tiles)
+            return rows[:].bitcast(F32).rearrange("p (a q u) -> p a u q", a=tiles, u=2)
 
         def words_by_column(grouped):
             return grouped[:].bitcast(F32).rearrange("p (c u) -> p c u", u=2)
@@ -92,6 +97,12 @@ def tile_differ_amplifier_pa_kernel(tc, h, w, w_ff, b_ff, out):
             return grouped[:].rearrange("p (c t) -> p c t", t=PACK)
 
         h_by_value = h_sb[:].rearrange("p (a q t) -> p a t q", a=ITEM_TILES, t=PACK)
+
+        h_words = keep.tile([P, ITEM_TILES, 2, P], F32)
+
+        def split_words(c):
+            tiles = slice(2 * c, 2 * c + 2)
+            nc.vector.tensor_copy(out=h_words[:, tiles, :, :], in_=words_by_tile(h_sb, ITEM_TILES)[:, tiles, :, :])
 
         def column_sums(total, c):
             for a in (2 * c, 2 * c + 1):
@@ -194,14 +205,17 @@ def tile_differ_amplifier_pa_kernel(tc, h, w, w_ff, b_ff, out):
         out_rows = out.rearrange("(p a) o -> p a o", a=ITEM_TILES)
         activated = {}
 
-        def second_product_by_channel(g):
+        channel_products = {}
+
+        def second_product_by_channel(g, idle_matmuls=0):
             items = slice(g * PAIR, (g + 1) * PAIR)
-            act = keep.tile([P, PACK, PAIR], F32, name="act%d" % g)
+            channel_products[g] = []
             for half in range(2):
-                product = back.tile([P, 2, PAIR], F32, tag="bank")
+                product = back.tile([P, 2, PAIR], F32, tag="bank", name="by_channel")
+                if half == 0:
+                    keep_warm(product[:, 0, :P], idle_matmuls)
                 for i in range(2):
-                    t = 2 * half + i
-                    channels = slice(t * P, (t + 1) * P)
+                    channels = slice((2 * half + i) * P, (2 * half + i + 1) * P)
                     nc.tensor.matmul_mx(
                         out=product[:, i, :],
                         lhsT=wf_codes[:, channels].bitcast(FP8X4),
@@ -211,22 +225,26 @@ def tile_differ_amplifier_pa_kernel(tc, h, w, w_ff, b_ff, out):
                         start=True,
                         stop=True,
                     )
-                for i in range(2):
-                    t = 2 * half + i
-                    nc.scalar.activation(
-                        out=act[:, t, :], in_=product[:, i, :], func=ACT.Sigmoid, bias=bias_col[:, t : t + 1]
-                    )
-            activated[g] = act
+                channel_products[g].append(product)
+            activated[g] = keep.tile([P, PACK, PAIR], F32, name="act%d" % g)
+
+        def activate_channels(g, first, last):
+            for t in range(first, last):
+                nc.scalar.activation(
+                    out=activated[g][:, t, :],
+                    in_=channel_products[g][t // 2][:, t % 2, :],
+                    func=ACT.Sigmoid,
+                    bias=bias_col[:, t : t + 1],
+                )
 
         turned = {}
 
-        def turn(g):
-            for a in (2 * g, 2 * g + 1):
-                columns = slice((a - 2 * g) * P, (a - 2 * g + 1) * P)
-                rows = back.tile([P, PACK, P], F32, tag="bank")
-                for t in range(PACK):
-                    nc.tensor.transpose(rows[:, t, :], activated[g][:, t, columns], ident[:])
-                turned[a] = rows
+        def turn(a):
+            columns = slice(a % 2 * P, (a % 2 + 1) * P)
+            rows = back.tile([P, PACK, P], F32, tag="bank")
+            for t in range(PACK):
+                nc.tensor.transpose(rows[:, t, :], activated[a // 2][:, t, columns], ident[:])
+            turned[a] = rows
 
         def store_turned(a, copy):
             result = results.tile([P, OUT], F32)
@@ -238,9 +256,10 @@ def tile_differ_amplifier_pa_kernel(tc, h, w, w_ff, b_ff, out):
 
         second_products = {}
 
-        def second_product_by_item(a, pool):
+        def second_product_by_item(a, pool, idle_matmuls=0):
             items = slice(a * P, (a + 1) * P)
             product = pool.tile([P, OUT], F32, tag="bank")
+            keep_warm(product[:, :P], idle_matmuls)
             nc.tensor.matmul_mx(
                 out=product[:],
                 lhsT=n_codes[:, items].bitcast(FP8X4),
@@ -270,30 +289,34 @@ def tile_differ_amplifier_pa_kernel(tc, h, w, w_ff, b_ff, out):
         for i in range(3):
             nc.tensor.matmul(out=idle[:], lhsT=zeros[:], rhs=zeros[:], start=True, stop=True)
         total = front.tile([P, SUM_COLS], F32, tag="bank", name="total")
+        split_words(0)
         column_sums(total, 0)
-        h_bank_0 = transpose_pair(front, words_by_tile(h_sb, ITEM_TILES)[:, 0 : 2, :])
-        copy_grouped(h_bank_0, h_grouped, 0)
+        split_words(1)
         column_sums(total, 1)
+        h_bank_0 = transpose_pair(front, h_words[:, 0 : 2, :, :])
+        copy_grouped(h_bank_0, h_grouped, 0)
+        split_words(2)
         column_sums(total, 2)
+        split_words(3)
         column_sums(total, 3)
         nc.vector.tensor_scalar_mul(
             out=shift[:],
             in0=total[:].rearrange("p (t c) -> p t c", t=PACK)[:, :, 0],
             scalar1=-1.0 / (ITEMS - 1),
         )
-        h_bank_1 = transpose_pair(back, words_by_tile(h_sb, ITEM_TILES)[:, 2 : 4, :])
+        h_bank_1 = transpose_pair(back, h_words[:, 2 : 4, :, :])
         copy_grouped(h_bank_1, h_grouped, 1)
         centre(0, 2)
-        w_bank_0 = transpose_pair(front, words_by_tile(w_sb, HID_TILES)[:, 0 : 2, :])
+        w_bank_0 = transpose_pair(front, words_by_tile(w_sb, HID_TILES)[:, 0 : 2, :, :])
         copy_grouped(w_bank_0, w_grouped, 0)
-        w_bank_1 = transpose_pair(front, words_by_tile(w_sb, HID_TILES)[:, 2 : 4, :])
+        w_bank_1 = transpose_pair(front, words_by_tile(w_sb, HID_TILES)[:, 2 : 4, :, :])
         copy_grouped(w_bank_1, w_grouped, 1)
-        f_bank_0 = transpose_pair(front, words_by_tile(wf_sb, HID_TILES)[:, 0 : 2, :])
+        f_bank_0 = transpose_pair(front, words_by_tile(wf_sb, HID_TILES)[:, 0 : 2, :, :])
         copy_grouped(f_bank_0, wf_grouped, 0)
-        f_bank_1 = transpose_pair(front, words_by_tile(wf_sb, HID_TILES)[:, 2 : 4, :])
+        f_bank_1 = transpose_pair(front, words_by_tile(wf_sb, HID_TILES)[:, 2 : 4, :, :])
         copy_grouped(f_bank_1, wf_grouped, 1)
-        h_bank_3 = transpose_pair(back, words_by_tile(h_sb, ITEM_TILES)[:, 6 : 8, :])
-        h_bank_2 = transpose_pair(back, words_by_tile(h_sb, ITEM_TILES)[:, 4 : 6, :])
+        h_bank_3 = transpose_pair(back, h_words[:, 6 : 8, :, :])
+        h_bank_2 = transpose_pair(back, h_words[:, 4 : 6, :, :])
         centre(2, 2)
         centred_6 = centre_on_scalar(h_bank_3, 6, 2)
         interleave_on_gpsimd(centred_6, 6, 2)
@@ -313,15 +336,18 @@ def tile_differ_amplifier_pa_kernel(tc, h, w, w_ff, b_ff, out):
         residual_add(2)
         quantise_pair(0)
         second_product_by_channel(0)
+        activate_channels(0, 0, PACK)
         residual_add(3)
         quantise(r_grouped, r_codes, r_scales, 3 * PAIR, PAIR)
         first_product(6)
         quantise_pair(1)
         second_product_by_channel(1)
+        activate_channels(1, 0, PACK)
         first_product(7)
         centre(4, 1)
         residual_add(6)
         turn(0)
+        turn(1)
         store_turned(0, nc.scalar.copy)
         store_turned(1, nc.scalar.copy)
         quantise(r_grouped, r_codes, r_scales, 2 * PAIR, PAIR)
@@ -329,16 +355,18 @@ def tile_differ_amplifier_pa_kernel(tc, h, w, w_ff, b_ff, out):
         first_product(5)
         residual_add(7)
         quantise_pair(3)
+        turn(2)
+        store_turned(2, nc.scalar.copy)
         residual_add(4)
         second_product_by_item(6, front)
-        turn(1)
-        store_turned(2, nc.scalar.copy)
+        turn(3)
         store_turned(3, nc.scalar.copy)
         second_product_by_item(7, front)
         residual_add(5)
-        finish(6)
-        quantise_pair(2)
+        quantise(n_grouped, n_codes, n_scales, 4 * P, P)
         second_product_by_item(4, front)
+        finish(6)
+        quantise(n_grouped, n_codes, n_scales, 5 * P, P)
         second_product_by_item(5, front)
         finish(7)
         finish(4)

from contextlib import ExitStack

import concourse.mybir as mybir
from concourse.masks import make_identity

F32 = mybir.dt.float32
BF16 = mybir.dt.bfloat16
U32 = mybir.dt.uint32
U8 = mybir.dt.uint8
FP8X4 = mybir.dt.float8_e4m3fn_x4
ALU = mybir.AluOpType
ACT = mybir.ActivationFunctionType

P = 128
PACK = 4
ITEMS = 1024
HID = 512
OUT = 512
ITEM_TILES = ITEMS // P
HID_TILES = HID // P
PAIR = 2 * P
HALF = ITEMS // 2
WARM_MATMULS = 3
SUM_COLS = 32

FLOPS = 2 * ITEMS * HID * HID + 2 * ITEMS * HID * OUT


def tile_differ_amplifier_pa_kernel(tc, h, w, w_ff, b_ff, out):
    nc = tc.nc
    with ExitStack() as ctx:
        keep = ctx.enter_context(tc.tile_pool(name="keep", bufs=1))
        results = ctx.enter_context(tc.tile_pool(name="results", bufs=ITEM_TILES))
        middle = ctx.enter_context(tc.tile_pool(name="middle", bufs=2))
        front = ctx.enter_context(tc.psum_pool(name="front", bufs=4))
        back = ctx.enter_context(tc.psum_pool(name="back", bufs=4))
        ctx.enter_context(tc.manual_schedule())

        h_sb = keep.tile([P, ITEM_TILES * HID], BF16)
        h_rows = h.rearrange("(p a) k -> p (a k)", a=ITEM_TILES)
        for c in range(ITEM_TILES // 2):
            cols = slice(c * 2 * HID, (c + 1) * 2 * HID)
            nc.sync.dma_start(out=h_sb[:, cols], in_=h_rows[:, cols])
        w_sb = keep.tile([P, HID_TILES * HID], BF16)
        wf_sb = keep.tile([P, HID_TILES * HID], BF16)
        for rows, source in ((w_sb, w), (wf_sb, w_ff)):
            nc.sync.dma_start(out=rows[:], in_=source.rearrange("(p t) k -> p (t k)", t=PACK))
        bias_col = keep.tile([P, PACK], BF16)
        nc.sync.dma_start(out=bias_col[:], in_=b_ff.rearrange("(p t) -> p t", t=PACK))
        bias = keep.tile([P, OUT], BF16)
        nc.sync.dma_start(out=bias[:], in_=b_ff.partition_broadcast(P))

        zeros = keep.tile([P, P], F32)
        nc.vector.memset(zeros[:], 0.0)
        ident = keep.tile([P, P], F32)
        make_identity(nc, ident[:])
        pick = keep.tile([P, PACK, SUM_COLS], BF16)
        nc.vector.memset(pick[:], 0.0)
        for t in range(PACK):
            nc.vector.memset(pick[:, t, 8 * t : 8 * t + 8], 1.0)
        warm = keep.tile([P, 1], F32)
        nc.vector.memset(warm[:], 0.0)
        nc.scalar.activation(out=warm[:], in_=warm[:], func=ACT.Sigmoid)

        def transpose_pair(pool, rows_words, idle_matmuls=0):
            bank = pool.tile([P, 2, PAIR], F32, tag="bank", name="words")
            keep_warm(bank[:, 0, :P], idle_matmuls)
            for i in range(2):
                for u in range(2):
                    nc.tensor.transpose(bank[:, u, i * P : (i + 1) * P], rows_words[:, i, u, :], ident[:])
            return bank

        def keep_warm(bank, count):
            for i in range(count):
                nc.tensor.matmul(out=bank, lhsT=zeros[:], rhs=zeros[:], start=True, stop=True)

        def copy_grouped(bank, grouped, c):
            nc.scalar.copy(
                out=words_by_column(grouped)[:, c * PAIR : (c + 1) * PAIR, :],
                in_=bank[:].rearrange("p u c -> p c u"),
            )

        def quantise(grouped, codes, scales, first, count):
            nc.vector.quantize_mx(
                out=codes[:, first : first + count].bitcast(FP8X4),
                scales=scales[:, first : first + count],
                in_=grouped[:, PACK * first : PACK * (first + count)],
            )

        def words_by_tile(rows, tiles):
            return rows[:].bitcast(F32).rearrange("p (a q u) -> p a u q", a=tiles, u=2)

        def words_by_column(grouped):
            return grouped[:].bitcast(F32).rearrange("p (c u) -> p c u", u=2)

        def by_column(grouped):
            return grouped[:].rearrange("p (c t) -> p c t", t=PACK)

        h_by_value = h_sb[:].rearrange("p (a q t) -> p a t q", a=ITEM_TILES, t=PACK)

        h_words = keep.tile([P, ITEM_TILES, 2, P], F32)

        def split_words(c):
            tiles = slice(2 * c, 2 * c + 2)
            nc.vector.tensor_copy(out=h_words[:, tiles, :, :], in_=words_by_tile(h_sb, ITEM_TILES)[:, tiles, :, :])

        def column_sums(total, c):
            for a in (2 * c, 2 * c + 1):
                for t in range(PACK):
                    nc.tensor.matmul(
                        out=total[:],
                        lhsT=h_by_value[:, a, t, :],
                        rhs=pick[:, t, :],
                        start=(a == 0 and t == 0),
                        stop=(a == ITEM_TILES - 1 and t == PACK - 1),
                    )

        h_grouped = keep.tile([P, ITEMS * PACK], BF16, align_bytes=64)
        w_grouped = keep.tile([P, HID * PACK], BF16, align_bytes=64)
        wf_grouped = keep.tile([P, OUT * PACK], BF16, align_bytes=64)

        w_codes = keep.tile([P, HID], U32, align_bytes=64)
        w_scales = keep.tile([P, HID], U8, align_bytes=64)
        wf_codes = keep.tile([P, OUT], U32, align_bytes=64)
        wf_scales = keep.tile([P, OUT], U8, align_bytes=64)

        shift = keep.tile([P, PACK], F32)
        r_grouped = keep.tile([P, ITEMS * PACK], BF16, align_bytes=64)
        r_codes = keep.tile([P, ITEMS], U32, align_bytes=64)
        r_scales = keep.tile([P, ITEMS], U8, align_bytes=64)

        def centre(first, count):
            cols = slice(first * P, (first + count) * P)
            nc.vector.scalar_tensor_tensor(
                out=by_column(r_grouped)[:, cols, :],
                in0=by_column(h_grouped)[:, cols, :],
                scalar=ITEMS / (ITEMS - 1),
                in1=shift[:].unsqueeze(1).to_broadcast([P, count * P, PACK]),
                op0=ALU.mult,
                op1=ALU.add,
            )

        def centre_on_scalar(bank, first, count):
            centred = middle.tile([P, PACK, PAIR], BF16, name="centred")
            values = bank[:].rearrange("p u c -> p (u c)").bitcast(BF16).rearrange("p (u c e) -> p u e c", u=2, e=2)
            start = first % 2 * P
            for t in range(PACK):
                nc.scalar.activation(
                    out=centred[:, t, : count * P],
                    in_=values[:, t // 2, t % 2, start : start + count * P],
                    func=ACT.Identity,
                    scale=ITEMS / (ITEMS - 1),
                    bias=shift[:, t : t + 1],
                )
            return centred

        def interleave_on_gpsimd(centred, first, count):
            for i in range(count):
                items = slice((first + i) * P, (first + i + 1) * P)
                nc.gpsimd.tensor_scalar(
                    out=by_column(r_grouped)[:, items, :],
                    in0=centred[:, :, i * P : (i + 1) * P].rearrange("p t c -> p c t"),
                    scalar1=1.0,
                    scalar2=0.0,
                    op0=ALU.mult,
                    op1=ALU.add,
                )

        def interleave_on_scalar(centred, first, count):
            items = slice(first * P, (first + count) * P)
            nc.scalar.copy(
                out=by_column(r_grouped)[:, items, :], in_=centred[:, :, : count * P].rearrange("p t c -> p c t")
            )

        n_grouped = keep.tile([P, ITEMS * PACK], BF16, align_bytes=64)
        n_codes = keep.tile([P, ITEMS], U32, align_bytes=64)
        n_scales = keep.tile([P, ITEMS], U8, align_bytes=64)
        first_products = {}

        def first_product(a):
            items = slice(a * P, (a + 1) * P)
            product = front.tile([P, PACK, P], F32, tag="bank")
            for t in range(PACK):
                units = slice(t * P, (t + 1) * P)
                nc.tensor.matmul_mx(
                    out=product[:, t, :],
                    lhsT=w_codes[:, units].bitcast(FP8X4),
                    lhsT_scale=w_scales[:, units],
                    rhs=r_codes[:, items].bitcast(FP8X4),
                    rhs_scale=r_scales[:, items],
                    start=True,
                    stop=True,
                )
            first_products[a] = product

        def residual_add(a):
            items = slice(a * P, (a + 1) * P)
            nc.vector.tensor_tensor(
                out=by_column(n_grouped)[:, items, :],
                in0=first_products[a][:].rearrange("p t n -> p n t"),
                in1=by_column(h_grouped)[:, items, :],
                op=ALU.add,
            )

        out_rows = out.rearrange("(p a) o -> p a o", a=ITEM_TILES)
        activated = {}

        channel_products = {}

        def second_product_by_channel(g, idle_matmuls=0):
            items = slice(g * PAIR, (g + 1) * PAIR)
            channel_products[g] = []
            for half in range(2):
                product = back.tile([P, 2, PAIR], F32, tag="bank", name="by_channel")
                if half == 0:
                    keep_warm(product[:, 0, :P], idle_matmuls)
                for i in range(2):
                    channels = slice((2 * half + i) * P, (2 * half + i + 1) * P)
                    nc.tensor.matmul_mx(
                        out=product[:, i, :],
                        lhsT=wf_codes[:, channels].bitcast(FP8X4),
                        lhsT_scale=wf_scales[:, channels],
                        rhs=n_codes[:, items].bitcast(FP8X4),
                        rhs_scale=n_scales[:, items],
                        start=True,
                        stop=True,
                    )
                channel_products[g].append(product)
            activated[g] = keep.tile([P, PACK, PAIR], F32, name="act%d" % g)

        def activate_channels(g, first, last):
            for t in range(first, last):
                nc.scalar.activation(
                    out=activated[g][:, t, :],
                    in_=channel_products[g][t // 2][:, t % 2, :],
                    func=ACT.Sigmoid,
                    bias=bias_col[:, t : t + 1],
                )

        turned = {}

        def turn(a):
            columns = slice(a % 2 * P, (a % 2 + 1) * P)
            rows = back.tile([P, PACK, P], F32, tag="bank")
            for t in range(PACK):
                nc.tensor.transpose(rows[:, t, :], activated[a // 2][:, t, columns], ident[:])
            turned[a] = rows

        def store_turned(a, copy):
            result = results.tile([P, OUT], F32)
            copy(
                out=result[:].rearrange("p (m t) -> p m t", t=PACK),
                in_=turned[a][:].rearrange("p t m -> p m t"),
            )
            nc.sync.dma_start(out=out_rows[:, a, :], in_=result[:])

        second_products = {}

        def second_product_by_item(a, pool, idle_matmuls=0):
            items = slice(a * P, (a + 1) * P)
            product = pool.tile([P, OUT], F32, tag="bank")
            keep_warm(product[:, :P], idle_matmuls)
            nc.tensor.matmul_mx(
                out=product[:],
                lhsT=n_codes[:, items].bitcast(FP8X4),
                lhsT_scale=n_scales[:, items],
                rhs=wf_codes[:].bitcast(FP8X4),
                rhs_scale=wf_scales[:],
                start=True,
                stop=True,
            )
            second_products[a] = product

        def finish(a):
            result = results.tile([P, OUT], F32)
            nc.vector.tensor_tensor(
                out=result[:].rearrange("p (m t) -> p m t", t=PACK),
                in0=second_products[a][:].rearrange("p (t m) -> p m t", t=PACK),
                in1=bias[:].rearrange("p (m t) -> p m t", t=PACK),
                op=ALU.add,
            )
            nc.scalar.activation(out=result[:], in_=result[:], func=ACT.Sigmoid)
            nc.sync.dma_start(out=out_rows[:, a, :], in_=result[:])

        def quantise_pair(g):
            quantise(n_grouped, n_codes, n_scales, g * PAIR, PAIR)

        idle = front.tile([P, P], F32, tag="bank", name="idle")
        for i in range(3):
            nc.tensor.matmul(out=idle[:], lhsT=zeros[:], rhs=zeros[:], start=True, stop=True)
        total = front.tile([P, SUM_COLS], F32, tag="bank", name="total")
        split_words(0)
        column_sums(total, 0)
        split_words(1)
        column_sums(total, 1)
        h_bank_0 = transpose_pair(front, h_words[:, 0 : 2, :, :])
        copy_grouped(h_bank_0, h_grouped, 0)
        split_words(2)
        column_sums(total, 2)
        split_words(3)
        column_sums(total, 3)
        nc.vector.tensor_scalar_mul(
            out=shift[:],
            in0=total[:].rearrange("p (t c) -> p t c", t=PACK)[:, :, 0],
            scalar1=-1.0 / (ITEMS - 1),
        )
        h_bank_1 = transpose_pair(back, h_words[:, 2 : 4, :, :])
        copy_grouped(h_bank_1, h_grouped, 1)
        centre(0, 2)
        w_bank_0 = transpose_pair(front, words_by_tile(w_sb, HID_TILES)[:, 0 : 2, :, :])
        copy_grouped(w_bank_0, w_grouped, 0)
        w_bank_1 = transpose_pair(front, words_by_tile(w_sb, HID_TILES)[:, 2 : 4, :, :])
        copy_grouped(w_bank_1, w_grouped, 1)
        f_bank_0 = transpose_pair(front, words_by_tile(wf_sb, HID_TILES)[:, 0 : 2, :, :])
        copy_grouped(f_bank_0, wf_grouped, 0)
        f_bank_1 = transpose_pair(front, words_by_tile(wf_sb, HID_TILES)[:, 2 : 4, :, :])
        copy_grouped(f_bank_1, wf_grouped, 1)
        h_bank_3 = transpose_pair(back, h_words[:, 6 : 8, :, :])
        h_bank_2 = transpose_pair(back, h_words[:, 4 : 6, :, :])
        centre(2, 2)
        centred_6 = centre_on_scalar(h_bank_3, 6, 2)
        interleave_on_gpsimd(centred_6, 6, 2)
        quantise(w_grouped, w_codes, w_scales, 0, HID)
        quantise(r_grouped, r_codes, r_scales, 0, HALF)
        first_product(0)
        first_product(1)
        first_product(2)
        first_product(3)
        quantise(wf_grouped, wf_codes, wf_scales, 0, OUT)
        copy_grouped(h_bank_2, h_grouped, 2)
        copy_grouped(h_bank_3, h_grouped, 3)
        centred_t5 = centre_on_scalar(h_bank_2, 5, 1)
        interleave_on_scalar(centred_t5, 5, 1)
        residual_add(0)
        residual_add(1)
        residual_add(2)
        quantise_pair(0)
        second_product_by_channel(0)
        activate_channels(0, 0, PACK)
        residual_add(3)
        quantise(r_grouped, r_codes, r_scales, 3 * PAIR, PAIR)
        first_product(6)
        quantise_pair(1)
        second_product_by_channel(1)
        activate_channels(1, 0, PACK)
        first_product(7)
        centre(4, 1)
        residual_add(6)
        turn(0)
        turn(1)
        store_turned(0, nc.scalar.copy)
        store_turned(1, nc.scalar.copy)
        quantise(r_grouped, r_codes, r_scales, 2 * PAIR, PAIR)
        first_product(4)
        first_product(5)
        residual_add(7)
        quantise_pair(3)
        turn(2)
        store_turned(2, nc.scalar.copy)
        residual_add(4)
        second_product_by_item(6, front)
        turn(3)
        store_turned(3, nc.scalar.copy)
        second_product_by_item(7, front)
        residual_add(5)
        quantise(n_grouped, n_codes, n_scales, 4 * P, P)
        second_product_by_item(4, front)
        finish(6)
        quantise(n_grouped, n_codes, n_scales, 5 * P, P)
        second_product_by_item(5, front)
        finish(7)
        finish(4)
        finish(5)
